import numpy as np
import ml_dtypes

BF16 = ml_dtypes.bfloat16


def bf(x):
    return np.asarray(x, np.float32).astype(BF16)


def f32(x):
    return np.asarray(x, np.float32)


def f64(x):
    return np.asarray(x).astype(np.float64)


def striped(idx):
    return np.tile(idx.reshape(-1, 16).T, (8, 1))


V, D, M, N = 2048, 128, 256, 1024
SCALE = 1.0 / np.sqrt(D)


def sigmoid(z):
    return 1.0 / (1.0 + np.exp(-z))


def setup_inputs():
    return {"table": bf(np.random.standard_normal((V, D))), "pos": bf(0.5 * np.random.standard_normal((D, N))), "w": bf(0.5 * np.random.standard_normal((D, M))), "b": f32(0.1 * np.random.standard_normal((M, 1))), "offs": striped(np.random.permutation(np.tile(np.arange(V), 2))[:N])}


def reference(table, pos, w, b, offs):
    idx = offs[:16].T.reshape(-1)
    z = SCALE * (f64(w).T @ f64(table)[idx].T + 2.0 * (f64(w).T @ f64(pos))) + f64(b)
    return np.concatenate([sigmoid(z[:D]), z[D:]], axis=0)

@@ -1,0 +1,100 @@
+import math
+
+import concourse.mybir as mybir
+from concourse.masks import make_identity
+
+V, D, M, N = 2048, 128, 256, 1024
+P = 128
+PIECE = 512
+HALVES = M // P
+GROUP = 512
+SCALE = 1.0 / math.sqrt(D)
+FLOPS = 2 * (2 * M * D * N)
+
+BF16, F32, U16 = mybir.dt.bfloat16, mybir.dt.float32, mybir.dt.uint16
+MULT, ADD = mybir.AluOpType.mult, mybir.AluOpType.add
+SIGMOID = mybir.ActivationFunctionType.Sigmoid
+
+
+def tile_decoderonlyaft_kernel(tc, table, pos, w, b, offs, out):
+    nc = tc.nc
+    with (
+        tc.tile_pool(name="held", bufs=1) as held,
+        tc.tile_pool(name="results", bufs=4) as results,
+        tc.psum_pool(name="flips", bufs=4) as flips,
+        tc.psum_pool(name="psum", bufs=1) as psum,
+    ):
+        identity = held.tile([P, P], BF16, name="identity")
+        make_identity(nc, identity[:])
+
+        weights = held.tile([D, M], BF16, name="weights")
+        nc.sync.dma_start(weights[:], w)
+        positions = held.tile([D, N], BF16, name="positions")
+        nc.scalar.dma_start(positions[:], pos)
+
+        rows = [held.tile([P, GROUP // P, D], BF16, name=f"rows{g}") for g in range(V // GROUP)]
+        for g in range(V // GROUP):
+            queue = nc.sync if g % 2 == 0 else nc.scalar
+            queue.dma_start(
+                rows[g][:],
+                table[g * GROUP : (g + 1) * GROUP, :].rearrange("(c p) d -> p c d", p=P),
+            )
+
+        offsets = held.tile([P, N // 16], U16, name="offsets")
+        nc.sync.dma_start(offsets[:], offs)
+        bias = [held.tile([P, 1], F32, name=f"bias{half}") for half in range(HALVES)]
+        for half in range(HALVES):
+            nc.sync.dma_start(bias[half][:], b[half * P : (half + 1) * P, :])
+
+        weights_twice = held.tile([D, M], BF16, name="weights_twice")
+        nc.vector.tensor_scalar(weights_twice[:], weights[:], 2.0, None, MULT)
+
+        blocks = [(piece, half) for piece in range(N // PIECE) for half in range(HALVES)]
+        sums = {
+            (piece, half): psum.tile([P, PIECE], F32, name=f"sum{piece}{half}")
+            for piece, half in blocks
+        }
+
+        for piece, half in blocks:
+            nc.tensor.matmul(
+                sums[piece, half][:],
+                weights_twice[:, half * P : (half + 1) * P],
+                positions[:, piece * PIECE : (piece + 1) * PIECE],
+                start=True,
+                stop=False,
+            )
+
+        words = held.tile([D, V], BF16, name="words")
+        for g in range(V // GROUP):
+            flipped = flips.tile([D, GROUP], BF16, name="flipped")
+            for c in range(GROUP // P):
+                nc.tensor.transpose(flipped[:, c * P : (c + 1) * P], rows[g][:, c, :], identity[:])
+            if g % 2 == 0:
+                nc.vector.tensor_copy(words[:, g * GROUP : (g + 1) * GROUP], flipped[:])
+            else:
+                nc.scalar.copy(words[:, g * GROUP : (g + 1) * GROUP], flipped[:])
+
+        for piece, half in blocks:
+            looked_up = words[:].indirect(
+                offsets[:, piece * (PIECE // 16) : (piece + 1) * (PIECE // 16)]
+            )
+            nc.tensor.matmul(
+                sums[piece, half][:],
+                weights[:, half * P : (half + 1) * P],
+                looked_up,
+                start=False,
+                stop=True,
+            )
+            result = results.tile([P, PIECE], F32, name="result")
+            if half == 0:
+                nc.scalar.activation(
+                    result[:], sums[piece, half][:], SIGMOID, bias=bias[half][:], scale=SCALE
+                )
+            else:
+                nc.vector.tensor_scalar(
+                    result[:], sums[piece, half][:], SCALE, bias[half][:], MULT, ADD
+                )
+            queue = nc.sync if half == 0 else nc.scalar
+            queue.dma_start(
+                out[half * P : (half + 1) * P, piece * PIECE : (piece + 1) * PIECE], result[:]
+            )

@@ -24,6 +24,11 @@ def tile_decoderonlyaft_kernel(tc, table, pos, w, b, offs, out):
         tc.psum_pool(name="flips", bufs=4) as flips,
         tc.psum_pool(name="psum", bufs=1) as psum,
     ):
+        primer = held.tile([P, 1], F32, name="primer")
+        nc.vector.memset(primer[:], 0.0)
+        primed = held.tile([P, 1], F32, name="primed")
+        nc.scalar.activation(primed[:], primer[:], SIGMOID)
+
         identity = held.tile([P, P], BF16, name="identity")
         make_identity(nc, identity[:])
 

@@ -8,6 +8,7 @@ P = 128
 PIECE = 512
 HALVES = M // P
 GROUP = 512
+WAKING = 5
 SCALE = 1.0 / math.sqrt(D)
 FLOPS = 2 * (2 * M * D * N)
 
@@ -59,6 +60,11 @@ def tile_decoderonlyaft_kernel(tc, table, pos, w, b, offs, out):
             (piece, half): psum.tile([P, PIECE], F32, name=f"sum{piece}{half}")
             for piece, half in blocks
         }
+
+        zeros = held.tile([P, PIECE], BF16, name="zeros")
+        nc.vector.memset(zeros[:], 0.0)
+        for turn in range(WAKING):
+            nc.tensor.matmul(sums[0, 0][:], zeros[:, 0:P], zeros[:], start=True, stop=True)
 
         for piece, half in blocks:
             nc.tensor.matmul(

import math

import concourse.mybir as mybir
from concourse.masks import make_identity

V, D, M, N = 2048, 128, 256, 1024
P = 128
PIECE = 512
HALVES = M // P
GROUP = 512
WAKING = 5
SCALE = 1.0 / math.sqrt(D)
FLOPS = 2 * (2 * M * D * N)

BF16, F32, U16 = mybir.dt.bfloat16, mybir.dt.float32, mybir.dt.uint16
MULT, ADD = mybir.AluOpType.mult, mybir.AluOpType.add
SIGMOID = mybir.ActivationFunctionType.Sigmoid


def tile_decoderonlyaft_kernel(tc, table, pos, w, b, offs, out):
    nc = tc.nc
    with (
        tc.tile_pool(name="held", bufs=1) as held,
        tc.tile_pool(name="results", bufs=4) as results,
        tc.psum_pool(name="flips", bufs=4) as flips,
        tc.psum_pool(name="psum", bufs=1) as psum,
    ):
        primer = held.tile([P, 1], F32, name="primer")
        nc.vector.memset(primer[:], 0.0)
        primed = held.tile([P, 1], F32, name="primed")
        nc.scalar.activation(primed[:], primer[:], SIGMOID)

        identity = held.tile([P, P], BF16, name="identity")
        make_identity(nc, identity[:])

        weights = held.tile([D, M], BF16, name="weights")
        nc.sync.dma_start(weights[:], w)
        positions = held.tile([D, N], BF16, name="positions")
        nc.scalar.dma_start(positions[:], pos)

        rows = [held.tile([P, GROUP // P, D], BF16, name=f"rows{g}") for g in range(V // GROUP)]
        for g in range(V // GROUP):
            queue = nc.sync if g % 2 == 0 else nc.scalar
            queue.dma_start(
                rows[g][:],
                table[g * GROUP : (g + 1) * GROUP, :].rearrange("(c p) d -> p c d", p=P),
            )

        offsets = held.tile([P, N // 16], U16, name="offsets")
        nc.sync.dma_start(offsets[:], offs)
        bias = [held.tile([P, 1], F32, name=f"bias{half}") for half in range(HALVES)]
        for half in range(HALVES):
            nc.sync.dma_start(bias[half][:], b[half * P : (half + 1) * P, :])

        weights_twice = held.tile([D, M], BF16, name="weights_twice")
        nc.vector.tensor_scalar(weights_twice[:], weights[:], 2.0, None, MULT)

        blocks = [(piece, half) for piece in range(N // PIECE) for half in range(HALVES)]
        sums = {
            (piece, half): psum.tile([P, PIECE], F32, name=f"sum{piece}{half}")
            for piece, half in blocks
        }

        zeros = held.tile([P, PIECE], BF16, name="zeros")
        nc.vector.memset(zeros[:], 0.0)
        for turn in range(WAKING):
            nc.tensor.matmul(sums[0, 0][:], zeros[:, 0:P], zeros[:], start=True, stop=True)

        for piece, half in blocks:
            nc.tensor.matmul(
                sums[piece, half][:],
                weights_twice[:, half * P : (half + 1) * P],
                positions[:, piece * PIECE : (piece + 1) * PIECE],
                start=True,
                stop=False,
            )

        words = held.tile([D, V], BF16, name="words")
        for g in range(V // GROUP):
            flipped = flips.tile([D, GROUP], BF16, name="flipped")
            for c in range(GROUP // P):
                nc.tensor.transpose(flipped[:, c * P : (c + 1) * P], rows[g][:, c, :], identity[:])
            if g % 2 == 0:
                nc.vector.tensor_copy(words[:, g * GROUP : (g + 1) * GROUP], flipped[:])
            else:
                nc.scalar.copy(words[:, g * GROUP : (g + 1) * GROUP], flipped[:])

        for piece, half in blocks:
            looked_up = words[:].indirect(
                offsets[:, piece * (PIECE // 16) : (piece + 1) * (PIECE // 16)]
            )
            nc.tensor.matmul(
                sums[piece, half][:],
                weights[:, half * P : (half + 1) * P],
                looked_up,
                start=False,
                stop=True,
            )
            result = results.tile([P, PIECE], F32, name="result")
            if half == 0:
                nc.scalar.activation(
                    result[:], sums[piece, half][:], SIGMOID, bias=bias[half][:], scale=SCALE
                )
            else:
                nc.vector.tensor_scalar(
                    result[:], sums[piece, half][:], SCALE, bias[half][:], MULT, ADD
                )
            queue = nc.sync if half == 0 else nc.scalar
            queue.dma_start(
                out[half * P : (half + 1) * P, piece * PIECE : (piece + 1) * PIECE], result[:]
            )
